import numpy as np
import ml_dtypes


def mxq(x, axis, fmt="e4m3"):
    dtype, down = {"e4m3": (ml_dtypes.float8_e4m3fn, 7), "e5m2": (ml_dtypes.float8_e5m2, 14)}[fmt]
    v = np.moveaxis(np.asarray(x, np.float32).astype(ml_dtypes.bfloat16).astype(np.float64), axis, -1)
    blocks = v.reshape(v.shape[:-1] + (-1, 32))
    amax = np.abs(blocks).max(-1, keepdims=True)
    byte = np.maximum(np.where(amax > 0, np.frexp(amax)[1] - 1 + 127, 0) - down, 1)
    scale = np.exp2(byte - 127.0)
    codes = (blocks / scale).astype(np.float32).astype(dtype).astype(np.float64)
    return np.moveaxis((codes * scale).reshape(v.shape), -1, axis)


WIDE = False


def mx_kscale(k):
    if not WIDE:
        return np.ones(k)
    levels = np.array([10, -10, 5, -5, 0])
    if k % 512:
        return np.exp2(np.random.permutation(np.resize(levels, k // 32))).repeat(32)
    a = np.empty((k // 512, 16))
    for p in range(k // 512):
        a[p, :8] = np.random.permutation(np.resize(levels, 8))
        for g in range(8):
            far = levels[np.abs(levels - a[p, g]) >= 10]
            a[p, g + 8] = far[np.random.randint(len(far))]
    return np.exp2(a.ravel()).repeat(32)


BF16 = ml_dtypes.bfloat16


def bf(x):
    return np.asarray(x, np.float32).astype(BF16)


def f64(x):
    return np.asarray(x).astype(np.float64)


B, N, F, D = 8, 1024, 128, 256


def normalize_adjacency(adj):
    d = np.sum(adj, axis=-1)
    with np.errstate(divide="ignore"):
        d_sqrt_inv = np.power(d, -0.5)
    d_sqrt_inv = np.where(np.isinf(d_sqrt_inv), 0.0, d_sqrt_inv)
    return d_sqrt_inv[..., :, None] * adj * d_sqrt_inv[..., None, :]


def setup_inputs():
    s = mx_kscale(N)
    g = s.mean()
    return {"inputs": bf(np.random.standard_normal((B, N, F)) * (g / s)[:, None]),
            "adj": bf(np.random.uniform(size=(B, N, N)) * s),
            "W_kernel": bf(np.random.standard_normal((F, D)) * 0.2 * np.sqrt(N / F)),
            "W_bias": bf(np.random.standard_normal(D) * 0.2)}


def reference(inputs, adj, W_kernel, W_bias):
    adj_norm = normalize_adjacency(f64(adj))
    feats = f64(inputs) @ f64(W_kernel) + f64(W_bias)
    out = mxq(adj_norm, 2, "e4m3") @ mxq(feats, 1, "e4m3")
    return np.maximum(out, 0.0)

from contextlib import ExitStack

import concourse.mybir as mybir
from concourse.masks import make_identity

F32 = mybir.dt.float32
BF16 = mybir.dt.bfloat16
U32 = mybir.dt.uint32
U8 = mybir.dt.uint8
FP8X4 = mybir.dt.float8_e4m3fn_x4
ALU = mybir.AluOpType
ACT = mybir.ActivationFunctionType

B, N, F, D = 8, 1024, 128, 256
P = 128
TILES = N // P
GROUP = 4
LAST = B - 1
FLOPS = 2 * B * N * N * D + 2 * B * N * F * D


def tile_gcn_t_kernel(tc, inputs, adj, W_kernel, W_bias, out):
    nc = tc.nc
    with ExitStack() as ctx:
        ctx.enter_context(tc.manual_schedule())
        const = ctx.enter_context(tc.tile_pool(name="const", bufs=1))
        apool = ctx.enter_context(tc.tile_pool(name="apool", bufs=12))
        tpool = ctx.enter_context(tc.tile_pool(name="tpool", bufs=2 * GROUP))
        work = ctx.enter_context(tc.tile_pool(name="work", bufs=2))
        qpool = ctx.enter_context(tc.tile_pool(name="qpool", bufs=3))
        cpool = ctx.enter_context(tc.tile_pool(name="cpool", bufs=4))
        small = ctx.enter_context(tc.tile_pool(name="small", bufs=3))
        unread = ctx.enter_context(tc.tile_pool(name="unread", bufs=3))
        keep = ctx.enter_context(tc.tile_pool(name="keep", bufs=3))
        opool = ctx.enter_context(tc.tile_pool(name="opool", bufs=4))
        psum = ctx.enter_context(tc.psum_pool(name="psum", bufs=1))

        first_root = const.tile([P, 1], F32, name="first_root")
        nc.vector.memset(first_root[:], 1.0)
        nc.scalar.activation(out=first_root[:], in_=first_root[:], func=ACT.Sqrt)
        ident_b = const.tile([P, P], BF16, name="ident_b")
        make_identity(nc, ident_b[:])
        ident_f = const.tile([P, P], F32, name="ident_f")
        make_identity(nc, ident_f[:])
        w_sb = const.tile([P, D], BF16, name="w_sb")
        nc.sync.dma_start(out=w_sb[:], in_=W_kernel)
        bias_row = const.tile([P, D], BF16, name="bias_row")
        nc.vector.memset(bias_row[:], 0.0)
        ones_b = const.tile([P, P], BF16, name="ones_b")
        nc.vector.memset(ones_b[:], 1.0)
        bias_all = const.tile([P, P], BF16, name="bias_all")
        bias_col = const.tile([P, 1], F32, name="bias_col")
        x_sb = const.tile([P, 2 * B, 4, F], BF16, name="x_sb")
        x_hbm = inputs.rearrange("b n f -> (b n) f").rearrange("(q p t) f -> p q t f", p=P, t=4)

        st = {}
        plan = []

        def at(place, step, *args):
            plan.append((place, len(plan), step, args))

        def load_bias():
            nc.sync.dma_start(out=bias_row[0:1, :], in_=W_bias.unsqueeze(0))

        def load_x(i):
            nc.sync.dma_start(out=x_sb[:, 4 * i : 4 * i + 4], in_=x_hbm[:, 4 * i : 4 * i + 4])

        def load_adj(b, c):
            a_sb = apool.tile([P, 2, N], BF16, name="a_sb")
            rows = adj[b].rearrange("(g p t) m -> p g t m", p=P, t=4)
            g, t = divmod(2 * c, 4)
            if b == 0:
                for e in range(2):
                    nc.sync.dma_start(out=a_sb[:, e, :], in_=rows[:, g, t + e, :])
            else:
                nc.sync.dma_start(out=a_sb[:], in_=rows[:, g, t : t + 2, :])
            st["adj", b, c] = a_sb

        def bias_ready():
            spread = psum.tile([P, P], F32, name="spread", tag="xf", bufs=2)
            nc.tensor.matmul(spread[:], lhsT=ones_b[:], rhs=bias_row[:, 0:P], start=True, stop=True)
            nc.vector.tensor_copy(out=bias_all[:], in_=spread[:])
            turned = psum.tile([P, P], BF16, name="turned", tag="xf", bufs=2)
            nc.tensor.transpose(turned[:], bias_row[:, 0:P], ident_b[:])
            nc.vector.tensor_copy(out=bias_col[:], in_=turned[:, 0:1])

        def x_turn(b):
            xtp = psum.tile([P, TILES, P], BF16, name="xtp", tag="xf", bufs=2)
            for j in range(TILES):
                nc.tensor.transpose(xtp[:, j, :], x_sb[:, 2 * b + j // 4, j % 4, :], ident_b[:])
            st["xtp", b] = xtp

        def x_copy(b):
            xt = work.tile([P, TILES, P], BF16, name="xt")
            nc.scalar.copy(out=xt[:], in_=st["xtp", b][:])
            st["xt", b] = xt

        def bias_in_psum(b, h):
            return h == 1 or b == LAST

        def feats_matmul(b, g, h):
            fp = psum.tile([P, 4, P], F32, name="fp", tag="xf", bufs=2)
            open_group = bias_in_psum(b, h)
            if h == 1:
                nc.tensor.matmul(
                    fp[:],
                    lhsT=ones_b[:],
                    rhs=bias_row[:, P:D].unsqueeze(1).to_broadcast([P, 4, P]),
                    start=True,
                    stop=False,
                )
            elif open_group:
                for t in range(4):
                    nc.tensor.matmul(
                        fp[:, t, :],
                        lhsT=bias_col[:].to_broadcast([P, P]),
                        rhs=ident_f[:],
                        is_transpose=True,
                        start=(t == 0),
                        stop=False,
                    )
            for t in range(4):
                nc.tensor.matmul(
                    fp[:, t, :],
                    lhsT=st["xt", b][:, 4 * g + t, :],
                    rhs=w_sb[:, h * P : (h + 1) * P],
                    start=not open_group,
                    stop=not open_group or t == 3,
                )
            st["fp", b, g, h] = fp

        def feats_out(b, g, h):
            if ("feats", b) not in st:
                feats = work.tile([P, 2, D, 4], BF16, name="feats", align_bytes=64)
                st["feats", b] = feats
            grouped = st["feats", b][:, g, h * P : (h + 1) * P, :]
            raw = st["fp", b, g, h][:].rearrange("p t d -> p d t")
            if bias_in_psum(b, h):
                nc.scalar.activation(out=grouped, in_=raw, func=ACT.Copy)
            else:
                nc.vector.tensor_tensor(
                    out=grouped,
                    in0=raw,
                    in1=bias_all[:].unsqueeze(2).to_broadcast([P, P, 4]),
                    op=ALU.add,
                )

        def feats_quantize(b):
            codes = keep.tile([P, 2 * D], U32, name="f_codes", align_bytes=64)
            scales = keep.tile([P, 2 * D], U8, name="f_scales", align_bytes=64)
            nc.vector.quantize_mx(
                out=codes[:].bitcast(FP8X4),
                scales=scales[:],
                in_=st["feats", b][:].rearrange("p g d t -> p (g d t)"),
            )
            st["f_mx", b] = (codes, scales)

        def row_sum(b, j, engine):
            row = st["adj", b, j // 2][:, j % 2, :]
            if ("d", b) not in st:
                d_new = small.tile([P, TILES], F32, name="d")
                st["d", b] = d_new
            total = st["d", b][:, j : j + 1]
            if engine == "vector":
                by_vector = unread.tile([P, N], BF16, name="by_vector")
                nc.vector.tensor_scalar(
                    out=by_vector[:],
                    in0=row,
                    scalar1=1.0,
                    scalar2=None,
                    op0=ALU.mult,
                    op1=ALU.add,
                    accum_out=total,
                )
            else:
                by_scalar = unread.tile([P, N], BF16, name="by_scalar")
                nc.scalar.activation(out=by_scalar[:], in_=row, func=ACT.Copy, accum_out=total)

        def root(b, c0, c1):
            if c0 == 0:
                for name in ("root", "inverse", "live", "r"):
                    column = small.tile([P, TILES], F32, name="column", tag=name)
                    st[name, b] = column
            nc.scalar.activation(
                out=st["root", b][:, c0:c1], in_=st["d", b][:, c0:c1], func=ACT.Sqrt, bias=1e-30
            )

        def invert(b, c0, c1):
            nc.vector.reciprocal(out=st["inverse", b][:, c0:c1], in_=st["root", b][:, c0:c1])

        def mask(b, c0, c1):
            live = st["live", b][:, c0:c1]
            nc.gpsimd.tensor_scalar(
                out=live,
                in0=st["d", b][:, c0:c1],
                scalar1=0.0,
                scalar2=1.0,
                op0=ALU.is_gt,
                op1=ALU.mult,
            )
            nc.gpsimd.tensor_tensor(
                out=st["r", b][:, c0:c1], in0=st["inverse", b][:, c0:c1], in1=live, op=ALU.mult
            )

        def rows_new(b, j):
            rows = tpool.tile([P, 4, 2 * P], F32, name="rows")
            st["rows", b, j] = rows

        def let_go(b, j):
            rows_new(b, j)
            nc.vector.memset(st["rows", b, j][:, 0, 0:1], 0.0)

        def scale_rows(b, j, engine):
            if ("rows", b, j) not in st:
                rows_new(b, j)
            rows = st["rows", b, j][:].rearrange("q t (c i) -> q c t i", i=4)
            a = st["adj", b, j // 2][:, j % 2, :].rearrange("q (c i t) -> q c t i", t=4, i=4)
            r_n = st["r", b][:, j : j + 1]
            if engine == "gpsimd":
                nc.gpsimd.tensor_scalar(
                    out=rows, in0=a, scalar1=r_n, scalar2=0.0, op0=ALU.mult, op1=ALU.add
                )
            elif engine == "vector":
                nc.vector.tensor_scalar_mul(out=rows, in0=a, scalar1=r_n)
            else:
                nc.scalar.activation(out=rows, in_=a, func=ACT.Copy, scale=r_n)

        def turn(b, j, g):
            tp = psum.tile([P, 4, P], F32, name="tp", tag="w", bufs=4)
            rows = st["rows", b, j]
            for t in range(4):
                nc.tensor.transpose(tp[:, t, :], rows[:, t, g * P : (g + 1) * P], ident_f[:])
            st["tp", b, j, g] = tp

        def widths(b):
            return (GROUP, GROUP) if b < LAST else (GROUP, 2, 1, 1)

        def group_of(b, j):
            k, start = 0, 0
            while j >= start + widths(b)[k]:
                start += widths(b)[k]
                k += 1
            return k, j - start, widths(b)[k]

        def scale_columns(b, j, g):
            k, rank, width = group_of(b, j)
            if g == 0 and rank == 0:
                grouped = qpool.tile([P, width, 2, P, 4], BF16, name="grouped", align_bytes=64)
                st["grouped", b, k] = grouped
            nc.vector.tensor_tensor(
                out=st["grouped", b, k][:, rank, g, :, :],
                in0=st["tp", b, j, g][:].rearrange("p t n -> p n t"),
                in1=st["r", b][:, 4 * g : 4 * g + 4].unsqueeze(1).to_broadcast([P, P, 4]),
                op=ALU.mult,
            )

        def quantize(b, k):
            width = widths(b)[k]
            codes = cpool.tile([P, width * 2 * P], U32, name="a_codes", align_bytes=64)
            scales = cpool.tile([P, width * 2 * P], U8, name="a_scales", align_bytes=64)
            nc.vector.quantize_mx(
                out=codes[:].bitcast(FP8X4),
                scales=scales[:],
                in_=st["grouped", b, k][:].rearrange("p e g n t -> p (e g n t)"),
            )
            st["a_mx", b, k] = (codes, scales)

        def multiply(b, j):
            k, rank, width = group_of(b, j)
            a_codes, a_scales = st["a_mx", b, k]
            f_codes, f_scales = st["f_mx", b]
            e = j % 2
            if e == 0:
                both = psum.tile([P, 2, D], F32, name="both", tag="o", bufs=2)
                st["both", b, j // 2] = both
            result = st["both", b, j // 2][:, e, :]
            if e == 1:
                nc.tensor.matmul_mx(
                    out=result,
                    lhsT=f_codes[:, 0:P].bitcast(FP8X4),
                    lhsT_scale=f_scales[:, 0:P],
                    rhs=f_codes[:, D : 2 * D].bitcast(FP8X4),
                    rhs_scale=f_scales[:, D : 2 * D],
                    start=True,
                    stop=True,
                )
            for g in range(2):
                c0 = (2 * rank + g) * P
                nc.tensor.matmul_mx(
                    out=result,
                    lhsT=a_codes[:, c0 : c0 + P].bitcast(FP8X4),
                    lhsT_scale=a_scales[:, c0 : c0 + P],
                    rhs=f_codes[:, g * D : (g + 1) * D].bitcast(FP8X4),
                    rhs_scale=f_scales[:, g * D : (g + 1) * D],
                    start=(g == 0),
                    stop=(g == 1),
                )

        def relu_store(b, j0, j1):
            relu = opool.tile([P, 2, D], F32, name="relu")
            part = slice(j0 % 2, j0 % 2 + j1 - j0)
            nc.scalar.activation(
                out=relu[:, part, :], in_=st["both", b, j0 // 2][:, part, :], func=ACT.Relu
            )
            out_rows = out[b].rearrange("(g p t) d -> p g t d", p=P, t=4)
            t0 = j0 % 4
            nc.sync.dma_start(out=out_rows[:, j0 // 4, t0 : t0 + j1 - j0, :], in_=relu[:, part, :])


        at(-100, load_adj, 0, 0)
        at(-100, load_bias)
        for c in range(1, 4):
            at(-100, load_adj, 0, c)
        at(-100, load_x, 0)
        for c in range(4):
            at(-100, load_adj, 1, c)
        for b in range(2, B):
            if b % 2 == 0:
                at(TILES * b - 18, load_x, b // 2)
            for c in range(4):
                at(TILES * b - 18 + 2 * c, load_adj, b, c)

        at(-50, bias_ready)
        for j in range(TILES):
            at(-40 + j, row_sum, 0, j, "vector" if j % 2 else "scalar")
        at(-37, root, 0, 0, 4)
        at(-35, invert, 0, 0, 4)
        at(-33, root, 0, 4, 8)
        at(-33, invert, 0, 4, 8)
        at(-32, mask, 0, 0, 4)
        at(-32, scale_rows, 0, 0, "gpsimd")
        at(-32, mask, 0, 4, 8)
        for j in range(1, 7):
            at(-32, scale_rows, 0, j, "gpsimd")
        at(-32, x_turn, 0)
        at(-32, x_copy, 0)
        for g in range(2):
            at(-32, turn, 0, 0, g)
        at(-31, x_turn, 1)

        last_sum = TILES * LAST - 6.5
        for b in range(B):
            first = TILES * b

            if b > 0:
                for j in range(TILES):
                    if b == 1 and j % 2 == 1:
                        at((j - 1) / 4, row_sum, b, j, "vector")
                    else:
                        at(first - 13.5 + j, row_sum, b, j, "scalar")
                    if b == 1 and j == 0:
                        at(first - 13.5, x_copy, 1)
                at(first - 6.5, root, b, 0, TILES)
                at(first - 4.5, invert, b, 0, TILES)
                at(first - 4.5, mask, b, 0, TILES)

            if b > 1:
                at(first - 7.5, x_turn, b)
                at(first - 6.5, x_copy, b)
            if b > 0:
                for g in range(2):
                    for h in range(2):
                        at(first - 6 + 4 * g, feats_matmul, b, g, h)
                        at(first - 4 + 4 * g, feats_out, b, g, h)
            else:
                at(-3, feats_matmul, 0, 0, 0)
                at(-0.25, feats_matmul, 0, 0, 1)
                at(0.25, feats_out, 0, 0, 1)
                at(0.5, feats_out, 0, 0, 0)
                at(1.25, feats_matmul, 0, 1, 0)
                at(1.25, feats_matmul, 0, 1, 1)
                at(2.5, feats_out, 0, 1, 1)
                at(3, feats_out, 0, 1, 0)

            for j in range(TILES):
                i = first + j
                k, rank, width = group_of(b, j)
                for g in range(2):
                    if i > 0:
                        at(i - 1.5, turn, b, j, g)
                    at(i + 0.5 * g, scale_columns, b, j, g)
                if rank < width - 1:
                    continue
                end = i + 0.75
                if width == GROUP:
                    nxt = i + GROUP
                    if nxt < B * TILES:
                        by_scalar = nxt % 16 == 15 or end > last_sum
                        at(end, scale_rows, nxt // 8, nxt % 8, "scalar" if by_scalar else "vector")
                    if k == 0:
                        at(end, feats_quantize, b)
                    burst = [i + GROUP + 1 + q for q in range(3) if i + GROUP + 1 < B * TILES]
                    if burst:
                        at(end, let_go, burst[0] // 8, burst[0] % 8)
                    at(end, quantize, b, k)
                    for q in burst:
                        at(end, scale_rows, q // 8, q % 8, "gpsimd")
                else:
                    end = i + (0.75 if i == B * TILES - 1 else 1.25)
                    at(end, quantize, b, k)
                for e in range(width):
                    jm = j - rank + e
                    go = end + 0.25 + 2 * (e // 2)
                    at(go, multiply, b, jm)
                    leave = go + (2 if b < LAST else 0.25)
                    if b * TILES + jm >= B * TILES - 2:
                        at(leave, relu_store, b, jm, jm + 1)
                    elif jm % 2 == 1:
                        at(leave, relu_store, b, jm - 1, jm + 1)

        for place, order, step, args in sorted(plan, key=lambda item: item[:2]):
            step(*args)
